import numpy as np
import ml_dtypes


def mxq(x, axis, fmt="e4m3"):
    dtype, down = {"e4m3": (ml_dtypes.float8_e4m3fn, 7), "e5m2": (ml_dtypes.float8_e5m2, 14)}[fmt]
    v = np.moveaxis(np.asarray(x, np.float32).astype(ml_dtypes.bfloat16).astype(np.float64), axis, -1)
    blocks = v.reshape(v.shape[:-1] + (-1, 32))
    amax = np.abs(blocks).max(-1, keepdims=True)
    byte = np.maximum(np.where(amax > 0, np.frexp(amax)[1] - 1 + 127, 0) - down, 1)
    scale = np.exp2(byte - 127.0)
    codes = (blocks / scale).astype(np.float32).astype(dtype).astype(np.float64)
    return np.moveaxis((codes * scale).reshape(v.shape), -1, axis)


WIDE = False


def mx_kscale(k):
    if not WIDE:
        return np.ones(k)
    levels = np.array([10, -10, 5, -5, 0])
    if k % 512:
        return np.exp2(np.random.permutation(np.resize(levels, k // 32))).repeat(32)
    a = np.empty((k // 512, 16))
    for p in range(k // 512):
        a[p, :8] = np.random.permutation(np.resize(levels, 8))
        for g in range(8):
            far = levels[np.abs(levels - a[p, g]) >= 10]
            a[p, g + 8] = far[np.random.randint(len(far))]
    return np.exp2(a.ravel()).repeat(32)


BF16 = ml_dtypes.bfloat16


def bf(x):
    return np.asarray(x, np.float32).astype(BF16)


def f64(x):
    return np.asarray(x).astype(np.float64)


B, S, DIM, HID, R, NT = 8, 64, 1024, 2560, 128, 3
SCALING = 4.0


def silu(v):
    return v / (1.0 + np.exp(-v))


def lora_out(xa, bw, tw):
    return (xa @ bw) * SCALING * tw[..., None]


def setup_inputs():
    s = mx_kscale(DIM)
    return {"x": bf(np.random.standard_normal((B, S, DIM)) * s),
            "w1": bf(np.random.standard_normal((DIM, HID)) / np.sqrt(DIM) / s[:, None]),
            "w3": bf(np.random.standard_normal((DIM, HID)) / np.sqrt(DIM) / s[:, None]),
            "xa_up": bf(np.random.standard_normal((B, S, R))),
            "b_up": bf(np.random.standard_normal((R, HID)) * 0.2 / np.sqrt(R)),
            "xa_gate": bf(np.random.standard_normal((B, S, R))),
            "b_gate": bf(np.random.standard_normal((R, HID)) * 0.2 / np.sqrt(R)),
            "tw_up": bf(np.random.uniform(size=(B, S))),
            "tw_gate": bf(np.random.uniform(size=(B, S)))}


def core(x, w1, w3, xa_up, b_up, xa_gate, b_gate, tw_up, tw_gate):
    xq = mxq(f64(x), 2, "e4m3")
    up = (xq @ mxq(f64(w3), 0, "e4m3")) + lora_out(f64(xa_up), f64(b_up), f64(tw_up))
    gate = silu((xq @ mxq(f64(w1), 0, "e4m3")) + lora_out(f64(xa_gate), f64(b_gate), f64(tw_gate)))
    return gate * up


def e4m3fn_bytes(y):
    return np.clip(np.asarray(y, np.float64), -448.0, 448.0).astype(np.float32).astype(ml_dtypes.float8_e4m3fn).view(np.uint8)


def reference(x, w1, w3, xa_up, b_up, xa_gate, b_gate, tw_up, tw_gate):
    out = core(x, w1, w3, xa_up, b_up, xa_gate, b_gate, tw_up, tw_gate)
    s = np.max(np.abs(out), axis=-1, keepdims=True) / 448.0
    return out, e4m3fn_bytes(out / s)

@@ -1,0 +1,468 @@
+from contextlib import ExitStack
+
+import concourse.mybir as mybir
+from concourse.masks import make_identity
+
+F32 = mybir.dt.float32
+BF16 = mybir.dt.bfloat16
+U32 = mybir.dt.uint32
+U8 = mybir.dt.uint8
+FP8X4 = mybir.dt.float8_e4m3fn_x4
+FP8 = mybir.dt.float8_e4m3fn
+ACT = mybir.ActivationFunctionType
+ALU = mybir.AluOpType
+AX = mybir.AxisListType
+
+P = 128
+TOK = 512
+DIM = 1024
+HID = 2560
+RANK = 128
+TT = TOK // P
+NT = 512
+NJ = HID // NT
+NG = DIM // 512
+NU = 2 * NG
+NTILE = NJ * TT
+NUNIT = NJ * NU
+RAW_BUFS = 8
+GRP_BUFS = 2
+HEAD_UNITS = 6
+HEAD_V = 336
+STEADY_V = 0
+STEADY_G = 256
+CAST_V = (512, 512, 1024, 1664)
+
+G_PRODUCTS = (15, 16, 17, 18)
+
+PASS_FIRST = 6
+PASS_UNITS = 10
+
+FLOPS = 2 * TOK * DIM * HID * 2 + 2 * TOK * RANK * HID * 2
+
+
+def tile_feedforward_pa_kernel(
+    tc, x, w1, w3, xa_up, b_up, xa_gate, b_gate, tw_up, tw_gate, out_0, out_1
+):
+    nc = tc.nc
+    xf = x.flatten_outer_dims()
+    o0 = out_0.flatten_outer_dims()
+    o1 = out_1.flatten_outer_dims()
+
+    with ExitStack() as ctx:
+        const = ctx.enter_context(tc.tile_pool(name="const", bufs=1))
+        rawp = ctx.enter_context(tc.tile_pool(name="rawp", bufs=RAW_BUFS))
+        grpp = ctx.enter_context(tc.tile_pool(name="grpp", bufs=GRP_BUFS))
+        codep = ctx.enter_context(tc.tile_pool(name="codep", bufs=3))
+        lorap = ctx.enter_context(tc.tile_pool(name="lorap", bufs=4))
+        epi = ctx.enter_context(tc.tile_pool(name="epi", bufs=3))
+        o8p = ctx.enter_context(tc.tile_pool(name="o8p", bufs=4))
+        psum = ctx.enter_context(tc.psum_pool(name="psum", bufs=2))
+        ctx.enter_context(tc.manual_schedule())
+
+        zeros = const.tile([P, 1], F32, name="zeros")
+        junk = const.tile([P, 1], F32, name="junk")
+        ident_f = const.tile([P, P], F32, name="ident_f")
+        ident_b = const.tile([P, P], BF16, name="ident_b")
+        twr = const.tile([P, P], BF16, name="twr")
+        xag = const.tile([P, TT, RANK], BF16, name="xag")
+        xau = const.tile([P, TT, RANK], BF16, name="xau")
+        x_sb = []
+        for tt in range(TT):
+            x_sb.append(const.tile([P, DIM], BF16, name="x_sb%d" % tt))
+        bg_sb = []
+        bu_sb = []
+        for j in range(NJ):
+            bg_sb.append(const.tile([P, NT], BF16, name="bg_sb%d" % j))
+            bu_sb.append(const.tile([P, NT], BF16, name="bu_sb%d" % j))
+        xg = const.tile([P, TT, NG, P, 4], BF16, name="xg", align_bytes=64)
+        xc = const.tile([P, TT, NG * P], U32, name="xc", align_bytes=64)
+        xs = const.tile([P, TT, NG * P], U8, name="xs", align_bytes=64)
+        xagT = const.tile([P, TT, P], BF16, name="xagT")
+        xauT = const.tile([P, TT, P], BF16, name="xauT")
+        s_all = const.tile([P, 8], F32, name="s_all")
+        h_all = const.tile([P, TT, HID], F32, name="h_all")
+        stats = const.tile([P, TT, 8], F32, name="stats")
+        amax = const.tile([P, TT], F32, name="amax")
+        rcp = const.tile([P, TT], F32, name="rcp")
+        rsc = const.tile([P, TT], F32, name="rsc")
+
+        raw = {}
+        grp = {}
+        wc = {}
+        ws = {}
+        ps_l = {}
+        ps_u = {}
+        sb = {}
+        o8 = {}
+
+        def load_x(tt):
+            nc.sync.dma_start(out=x_sb[tt][:], in_=xf[tt * P : (tt + 1) * P, :])
+
+        def load_unit(q):
+            j, u = divmod(q, NU)
+            w = w1 if u < NG else w3
+            g = u % NG
+            t = rawp.tile([P, 4, NT], BF16, name="raw")
+            nc.sync.dma_start(
+                out=t[:],
+                in_=w[g * 512 : (g + 1) * 512, j * NT : (j + 1) * NT].rearrange(
+                    "(p t) c -> p t c", t=4
+                ),
+            )
+            raw[q] = t
+
+        def load_b(eng, j):
+            eng.dma_start(out=bg_sb[j][:], in_=b_gate[:, j * NT : (j + 1) * NT])
+            eng.dma_start(out=bu_sb[j][:], in_=b_up[:, j * NT : (j + 1) * NT])
+
+        xts = {}
+
+        def x_transpose(tt):
+            xw = x_sb[tt][:].bitcast(F32)
+            xt = psum.tile([P, NG, 2, P], F32, name="xt", tag=("ug" if tt % 2 == 0 else "uu"))
+            xts[tt] = xt
+            for g in range(NG):
+                for u in range(2):
+                    nc.tensor.transpose(
+                        out=xt[:, g, u, :],
+                        in_=xw[:, 256 * g + u : 256 * (g + 1) : 2],
+                        identity=ident_f[:],
+                    )
+
+        def x_copy(tt):
+            nc.scalar.copy(
+                out=xg[:, tt, :, :, :].bitcast(F32),
+                in_=xts[tt][:].rearrange("p g u r -> p g r u"),
+            )
+
+        def quant_x(tt):
+            nc.vector.quantize_mx(
+                out=xc[:, tt, :].bitcast(FP8X4),
+                scales=xs[:, tt, :],
+                in_=xg[:, tt, :, :, :].rearrange("p g r t -> p (g r t)"),
+            )
+
+        def prep_adapters():
+            pg = psum.tile([P, TT, P], BF16, name="pg", tag="l", bufs=3)
+            pu = psum.tile([P, TT, P], BF16, name="pu", tag="l", bufs=3)
+            pw = psum.tile([P, P], BF16, name="pw", tag="l", bufs=3)
+            for tt in range(TT):
+                nc.tensor.transpose(out=pg[:, tt, :], in_=xag[:, tt, :], identity=ident_b[:])
+            for tt in range(TT):
+                nc.tensor.transpose(out=pu[:, tt, :], in_=xau[:, tt, :], identity=ident_b[:])
+            nc.tensor.transpose(out=pw[:], in_=twr[:], identity=ident_b[:])
+            nc.scalar.copy(out=xagT[:], in_=pg[:])
+            nc.scalar.copy(out=xauT[:], in_=pu[:])
+            nc.vector.tensor_scalar(
+                out=s_all[:], in0=pw[:, 0:8], scalar1=4.0, scalar2=None, op0=ALU.mult
+            )
+
+        def split(q):
+            if q < HEAD_UNITS:
+                return {"V": (0, HEAD_V), "G": (0, 0), "S": (HEAD_V, NT)}
+            return {
+                "V": (0, STEADY_V),
+                "G": (STEADY_V, STEADY_V + STEADY_G),
+                "S": (STEADY_V + STEADY_G, NT),
+            }
+
+        def interleave(q, who):
+            if q not in grp:
+                grp[q] = grpp.tile([P, NT, 4], BF16, name="grp", align_bytes=64)
+            c0, c1 = split(q)[who]
+            if c1 <= c0:
+                return
+            src = raw[q][:, :, c0:c1].rearrange("p t (c i) -> p c t i", i=4)
+            dst = grp[q][:, c0:c1, :].rearrange("p (c i) t -> p c t i", i=4)
+            if who == "V":
+                nc.vector.tensor_copy(out=dst, in_=src)
+            elif who == "S":
+                nc.scalar.copy(out=dst, in_=src)
+            else:
+                nc.gpsimd.tensor_scalar(
+                    out=grp[q][:, c0:c1, :],
+                    in0=raw[q][:, :, c0:c1].rearrange("p t c -> p c t"),
+                    scalar1=1.0,
+                    scalar2=0.0,
+                    op0=ALU.mult,
+                    op1=ALU.add,
+                )
+
+        pts = {}
+
+        def through(q):
+            return PASS_FIRST <= q < PASS_FIRST + PASS_UNITS
+
+        def pass_pe(q):
+            c0 = split(q)["S"][0]
+            pt = psum.tile([P, 2, P, 4], BF16, name="pt", tag="pt", bufs=1)
+            for k in range(2):
+                nc.tensor.matmul(
+                    out=pt[:, k, :, :],
+                    lhsT=ident_b[:],
+                    rhs=raw[q][:, :, c0 + k * P : c0 + (k + 1) * P].rearrange("p t c -> p c t"),
+                    start=True,
+                    stop=True,
+                )
+            pts[q] = pt
+
+        def pass_s(q):
+            if q not in grp:
+                grp[q] = grpp.tile([P, NT, 4], BF16, name="grp", align_bytes=64)
+            c0, c1 = split(q)["S"]
+            nc.scalar.copy(
+                out=grp[q][:, c0:c1, :].rearrange("p c t -> p (c t)"),
+                in_=pts[q][:].rearrange("p k c t -> p (k c t)"),
+            )
+
+        def quantize(q):
+            j, u = divmod(q, NU)
+            if u == 0:
+                wc[j] = codep.tile([P, NU, NT], U32, name="wc", align_bytes=64)
+                ws[j] = codep.tile([P, NU, NT], U8, name="ws", align_bytes=64)
+            nc.vector.quantize_mx(
+                out=wc[j][:, u, :].bitcast(FP8X4),
+                scales=ws[j][:, u, :],
+                in_=grp[q][:].rearrange("p c t -> p (c t)"),
+            )
+
+        def lora_pe(i):
+            j, tt = divmod(i, TT)
+            lg = psum.tile([P, NT], F32, name="lg", tag="l", bufs=3)
+            lu = psum.tile([P, NT], F32, name="lu", tag="l", bufs=3)
+            nc.tensor.matmul(out=lg[:], lhsT=xagT[:, tt, :], rhs=bg_sb[j][:], start=True, stop=True)
+            nc.tensor.matmul(out=lu[:], lhsT=xauT[:, tt, :], rhs=bu_sb[j][:], start=True, stop=True)
+            ps_l[i] = (lg, lu)
+
+        def mm(i):
+            j, tt = divmod(i, TT)
+            ug = psum.tile([P, NT], F32, name="ug", tag="ug")
+            uu = psum.tile([P, NT], F32, name="uu", tag="uu")
+            for half, acc in ((0, ug), (1, uu)):
+                for g in range(NG):
+                    nc.tensor.matmul_mx(
+                        out=acc[:],
+                        lhsT=xc[:, tt, g * P : (g + 1) * P].bitcast(FP8X4),
+                        lhsT_scale=xs[:, tt, g * P : (g + 1) * P],
+                        rhs=wc[j][:, half * NG + g, :].bitcast(FP8X4),
+                        rhs_scale=ws[j][:, half * NG + g, :],
+                        start=(g == 0),
+                        stop=(g == NG - 1),
+                    )
+            ps_u[i] = (ug, uu)
+
+        def s12(i):
+            tt = i % TT
+            lg, lu = ps_l[i]
+            ag = lorap.tile([P, NT], F32, name="ag")
+            au = lorap.tile([P, NT], F32, name="au")
+            nc.scalar.activation(out=ag[:], in_=lg[:], func=ACT.Copy, scale=s_all[:, 4 + tt : 5 + tt])
+            nc.scalar.activation(out=au[:], in_=lu[:], func=ACT.Copy, scale=s_all[:, tt : tt + 1])
+            sb[i] = {"ag": ag, "au": au}
+
+        def v1(i):
+            gt = epi.tile([P, NT], F32, name="gt")
+            nc.vector.tensor_tensor(out=gt[:], in0=ps_u[i][0][:], in1=sb[i]["ag"][:], op=ALU.add)
+            sb[i]["gt"] = gt
+
+        def s3(i):
+            sg = epi.tile([P, NT], F32, name="sg")
+            nc.scalar.activation(out=sg[:], in_=sb[i]["gt"][:], func=ACT.Silu)
+            sb[i]["sg"] = sg
+
+        def v2(i):
+            up = epi.tile([P, NT], F32, name="up")
+            nc.vector.tensor_tensor(out=up[:], in0=ps_u[i][1][:], in1=sb[i]["au"][:], op=ALU.add)
+            sb[i]["up"] = up
+
+        def v3(i):
+            j, tt = divmod(i, TT)
+            hs = h_all[:, tt, j * NT : (j + 1) * NT]
+            eng = nc.gpsimd if i in G_PRODUCTS else nc.vector
+            eng.tensor_tensor(out=hs, in0=sb[i]["up"][:], in1=sb[i]["sg"][:], op=ALU.mult)
+            nc.sync.dma_start(out=o0[tt * P : (tt + 1) * P, j * NT : (j + 1) * NT], in_=hs)
+
+        def v4(i):
+            j, tt = divmod(i, TT)
+            nc.vector.tensor_reduce(
+                out=stats[:, tt, j : j + 1],
+                in_=h_all[:, tt, j * NT : (j + 1) * NT],
+                axis=AX.X,
+                op=ALU.max,
+                apply_absolute_value=True,
+            )
+
+        def fin_a(tt):
+            nc.vector.tensor_reduce(
+                out=amax[:, tt : tt + 1], in_=stats[:, tt, 0:NJ], axis=AX.X, op=ALU.max
+            )
+
+        def fin_b(tt):
+            nc.vector.reciprocal(out=rcp[:, tt : tt + 1], in_=amax[:, tt : tt + 1])
+
+        def fin_c(tt):
+            nc.vector.tensor_scalar(
+                out=rsc[:, tt : tt + 1],
+                in0=rcp[:, tt : tt + 1],
+                scalar1=448.0,
+                scalar2=None,
+                op0=ALU.mult,
+            )
+
+        def cast_cols(tt):
+            return CAST_V[tt]
+
+        def cast_v(tt):
+            cv = cast_cols(tt)
+            o8[tt] = o8p.tile([P, HID], FP8, name="o8")
+            nc.vector.tensor_scalar(
+                out=o8[tt][:, 0:cv],
+                in0=h_all[:, tt, 0:cv],
+                scalar1=rsc[:, tt : tt + 1],
+                scalar2=None,
+                op0=ALU.mult,
+                saturate=False,
+            )
+
+        def cast_s(tt):
+            cv = cast_cols(tt)
+            nc.scalar.activation(
+                out=o8[tt][:, cv:HID],
+                in_=h_all[:, tt, cv:HID],
+                func=ACT.Identity,
+                scale=rsc[:, tt : tt + 1],
+                bias=zeros[:, 0:1],
+                saturate=False,
+            )
+            nc.sync.dma_start(out=o1[tt * P : (tt + 1) * P, :], in_=o8[tt][:].bitcast(U8))
+
+        nc.vector.memset(zeros[:], 0.0)
+        nc.gpsimd.memset(twr[:], 0.0)
+        nc.scalar.activation(out=junk[:], in_=zeros[:], func=ACT.Silu)
+        make_identity(nc, ident_f[:])
+        make_identity(nc, ident_b[:])
+
+        load_unit(0)
+        load_x(0)
+        load_unit(1)
+        nc.sync.dma_start(
+            out=xag[:], in_=xa_gate.flatten_outer_dims().rearrange("(t p) r -> p t r", p=P)
+        )
+        nc.sync.dma_start(
+            out=xau[:], in_=xa_up.flatten_outer_dims().rearrange("(t p) r -> p t r", p=P)
+        )
+        nc.sync.dma_start(out=twr[0:4, :], in_=tw_up.rearrange("(t h) s -> t (h s)", h=2))
+        nc.sync.dma_start(out=twr[4:8, :], in_=tw_gate.rearrange("(t h) s -> t (h s)", h=2))
+        load_unit(2)
+        load_b(nc.sync, 0)
+        load_unit(3)
+        load_x(1)
+        load_unit(4)
+        load_x(2)
+        load_unit(5)
+        load_x(3)
+        load_unit(6)
+        load_b(nc.sync, 1)
+        load_unit(7)
+
+        def ok(i):
+            return 0 <= i < NTILE
+
+        def last(i):
+            return NTILE - TT <= i < NTILE
+
+        def late(i):
+            return i + 5 < NUNIT
+
+        def next_load(q):
+            nq = q + RAW_BUFS
+            if nq < NUNIT:
+                load_unit(nq)
+                if nq % NU == 0:
+                    load_b(nc.sync, nq // NU)
+
+        interleave(0, "V")
+        interleave(0, "S")
+        next_load(0)
+        x_transpose(0)
+        x_copy(0)
+        quantize(0)
+        quant_x(0)
+        interleave(1, "V")
+        interleave(1, "S")
+        next_load(1)
+        prep_adapters()
+        quantize(1)
+        interleave(2, "V")
+        interleave(2, "S")
+        next_load(2)
+        lora_pe(0)
+        s12(0)
+        quantize(2)
+        interleave(3, "V")
+        interleave(3, "S")
+        next_load(3)
+        x_transpose(1)
+        x_copy(1)
+        lora_pe(1)
+        s12(1)
+        quantize(3)
+        quant_x(1)
+        mm(0)
+        lora_pe(2)
+        interleave(4, "V")
+        interleave(4, "G")
+        interleave(4, "S")
+        next_load(4)
+        v1(0)
+        for s in range(0, NTILE + 3):
+            qq = s + 4
+            qi = s + 5
+            if 1 <= s <= 2:
+                quant_x(s + 1)
+            if qq < NUNIT:
+                quantize(qq)
+            if ok(s - 1) and late(s - 1):
+                v3(s - 1)
+            if ok(s + 1):
+                mm(s + 1)
+            if s <= 1:
+                x_transpose(s + 2)
+            if qi < NUNIT:
+                if through(qi):
+                    pass_s(qi)
+                else:
+                    interleave(qi, "S")
+            if through(qi + 1):
+                pass_pe(qi + 1)
+            if ok(s + 3):
+                lora_pe(s + 3)
+            if ok(s):
+                s3(s)
+            if qi < NUNIT:
+                interleave(qi, "V")
+                interleave(qi, "G")
+            if ok(s):
+                v2(s)
+            if last(s - 2):
+                fin_c((s - 2) % TT)
+            if ok(s + 2):
+                s12(s + 2)
+            if s <= 1:
+                x_copy(s + 2)
+            if ok(s - 1):
+                v4(s - 1)
+            if last(s - 2):
+                cast_v((s - 2) % TT)
+                cast_s((s - 2) % TT)
+            if ok(s + 1):
+                v1(s + 1)
+            if last(s - 1):
+                fin_a((s - 1) % TT)
+            if qi < NUNIT:
+                next_load(qi)
+            if ok(s) and not late(s):
+                v3(s)
+            if last(s - 1):
+                fin_b((s - 1) % TT)

@@ -37,6 +37,7 @@ G_PRODUCTS = (15, 16, 17, 18)
 
 PASS_FIRST = 6
 PASS_UNITS = 10
+PASS_G = 128
 
 FLOPS = 2 * TOK * DIM * HID * 2 + 2 * TOK * RANK * HID * 2
 
@@ -158,9 +159,14 @@ def tile_feedforward_pa_kernel(
                 out=s_all[:], in0=pw[:, 0:8], scalar1=4.0, scalar2=None, op0=ALU.mult
             )
 
+        def through(q):
+            return PASS_FIRST <= q < PASS_FIRST + PASS_UNITS
+
         def split(q):
             if q < HEAD_UNITS:
                 return {"V": (0, HEAD_V), "G": (0, 0), "S": (HEAD_V, NT)}
+            if through(q):
+                return {"V": (0, 0), "G": (0, PASS_G), "S": (PASS_G, NT - 2 * P), "T": (NT - 2 * P, NT)}
             return {
                 "V": (0, STEADY_V),
                 "G": (STEADY_V, STEADY_V + STEADY_G),
@@ -191,11 +197,8 @@ def tile_feedforward_pa_kernel(
 
         pts = {}
 
-        def through(q):
-            return PASS_FIRST <= q < PASS_FIRST + PASS_UNITS
-
         def pass_pe(q):
-            c0 = split(q)["S"][0]
+            c0 = split(q)["T"][0]
             pt = psum.tile([P, 2, P, 4], BF16, name="pt", tag="pt", bufs=1)
             for k in range(2):
                 nc.tensor.matmul(
@@ -210,7 +213,7 @@ def tile_feedforward_pa_kernel(
         def pass_s(q):
             if q not in grp:
                 grp[q] = grpp.tile([P, NT, 4], BF16, name="grp", align_bytes=64)
-            c0, c1 = split(q)["S"]
+            c0, c1 = split(q)["T"]
             nc.scalar.copy(
                 out=grp[q][:, c0:c1, :].rearrange("p c t -> p (c t)"),
                 in_=pts[q][:].rearrange("p k c t -> p (k c t)"),
@@ -432,8 +435,7 @@ def tile_feedforward_pa_kernel(
             if qi < NUNIT:
                 if through(qi):
                     pass_s(qi)
-                else:
-                    interleave(qi, "S")
+                interleave(qi, "S")
             if through(qi + 1):
                 pass_pe(qi + 1)
             if ok(s + 3):

@@ -38,6 +38,8 @@ G_PRODUCTS = (15, 16, 17, 18)
 PASS_FIRST = 6
 PASS_UNITS = 10
 PASS_G = 128
+SPLIT_PRODUCTS = 10
+SPLIT_G = 256
 
 FLOPS = 2 * TOK * DIM * HID * 2 + 2 * TOK * RANK * HID * 2
 
@@ -282,8 +284,17 @@ def tile_feedforward_pa_kernel(
         def v3(i):
             j, tt = divmod(i, TT)
             hs = h_all[:, tt, j * NT : (j + 1) * NT]
-            eng = nc.gpsimd if i in G_PRODUCTS else nc.vector
-            eng.tensor_tensor(out=hs, in0=sb[i]["up"][:], in1=sb[i]["sg"][:], op=ALU.mult)
+            if i < SPLIT_PRODUCTS:
+                cv = NT - SPLIT_G
+                nc.vector.tensor_tensor(
+                    out=hs[:, 0:cv], in0=sb[i]["up"][:, 0:cv], in1=sb[i]["sg"][:, 0:cv], op=ALU.mult
+                )
+                nc.gpsimd.tensor_tensor(
+                    out=hs[:, cv:NT], in0=sb[i]["up"][:, cv:NT], in1=sb[i]["sg"][:, cv:NT], op=ALU.mult
+                )
+            else:
+                eng = nc.gpsimd if i in G_PRODUCTS else nc.vector
+                eng.tensor_tensor(out=hs, in0=sb[i]["up"][:], in1=sb[i]["sg"][:], op=ALU.mult)
             nc.sync.dma_start(out=o0[tt * P : (tt + 1) * P, j * NT : (j + 1) * NT], in_=hs)
 
         def v4(i):
@@ -426,6 +437,8 @@ def tile_feedforward_pa_kernel(
                 quant_x(s + 1)
             if qq < NUNIT:
                 quantize(qq)
+            if qi < NUNIT:
+                interleave(qi, "G")
             if ok(s - 1) and late(s - 1):
                 v3(s - 1)
             if ok(s + 1):
@@ -444,7 +457,6 @@ def tile_feedforward_pa_kernel(
                 s3(s)
             if qi < NUNIT:
                 interleave(qi, "V")
-                interleave(qi, "G")
             if ok(s):
                 v2(s)
             if last(s - 2):

@@ -37,9 +37,9 @@ G_PRODUCTS = (15, 16, 17, 18)
 
 PASS_FIRST = 6
 PASS_UNITS = 10
-PASS_G = 128
+PASS_G = 160
 SPLIT_PRODUCTS = 10
-SPLIT_G = 256
+SPLIT_G = 192
 
 FLOPS = 2 * TOK * DIM * HID * 2 + 2 * TOK * RANK * HID * 2
 

@@ -35,10 +35,12 @@ CAST_V = (512, 512, 1024, 1664)
 
 G_PRODUCTS = (15, 16, 17, 18)
 
-PASS_FIRST = 6
+PASS_FIRST = 10
 PASS_UNITS = 10
 PASS_G = 160
+SPLIT_FIRST = 4
 SPLIT_PRODUCTS = 10
+HOLD_STORES = 7
 SPLIT_G = 192
 
 FLOPS = 2 * TOK * DIM * HID * 2 + 2 * TOK * RANK * HID * 2
@@ -284,7 +286,7 @@ def tile_feedforward_pa_kernel(
         def v3(i):
             j, tt = divmod(i, TT)
             hs = h_all[:, tt, j * NT : (j + 1) * NT]
-            if i < SPLIT_PRODUCTS:
+            if SPLIT_FIRST <= i < SPLIT_FIRST + SPLIT_PRODUCTS:
                 cv = NT - SPLIT_G
                 nc.vector.tensor_tensor(
                     out=hs[:, 0:cv], in0=sb[i]["up"][:, 0:cv], in1=sb[i]["sg"][:, 0:cv], op=ALU.mult
@@ -295,7 +297,17 @@ def tile_feedforward_pa_kernel(
             else:
                 eng = nc.gpsimd if i in G_PRODUCTS else nc.vector
                 eng.tensor_tensor(out=hs, in0=sb[i]["up"][:], in1=sb[i]["sg"][:], op=ALU.mult)
-            nc.sync.dma_start(out=o0[tt * P : (tt + 1) * P, j * NT : (j + 1) * NT], in_=hs)
+            if i + 1 >= HOLD_STORES:
+                store(i)
+                if i + 1 - HOLD_STORES < HOLD_STORES - 1:
+                    store(i + 1 - HOLD_STORES)
+
+        def store(i):
+            j, tt = divmod(i, TT)
+            nc.sync.dma_start(
+                out=o0[tt * P : (tt + 1) * P, j * NT : (j + 1) * NT],
+                in_=h_all[:, tt, j * NT : (j + 1) * NT],
+            )
 
         def v4(i):
             j, tt = divmod(i, TT)

@@ -170,7 +170,7 @@ def tile_feedforward_pa_kernel(
             if q < HEAD_UNITS:
                 return {"V": (0, HEAD_V), "G": (0, 0), "S": (HEAD_V, NT)}
             if through(q):
-                return {"V": (0, 0), "G": (0, PASS_G), "S": (PASS_G, NT - 2 * P), "T": (NT - 2 * P, NT)}
+                return {"V": (PASS_G, PASS_G + 64), "G": (0, PASS_G), "S": (PASS_G + 64, NT - 2 * P), "T": (NT - 2 * P, NT)}
             return {
                 "V": (0, STEADY_V),
                 "G": (STEADY_V, STEADY_V + STEADY_G),
@@ -447,6 +447,8 @@ def tile_feedforward_pa_kernel(
             qi = s + 5
             if 1 <= s <= 2:
                 quant_x(s + 1)
+            if qi < NUNIT and through(qi):
+                interleave(qi, "V")
             if qq < NUNIT:
                 quantize(qq)
             if qi < NUNIT:
@@ -467,7 +469,7 @@ def tile_feedforward_pa_kernel(
                 lora_pe(s + 3)
             if ok(s):
                 s3(s)
-            if qi < NUNIT:
+            if qi < NUNIT and not through(qi):
                 interleave(qi, "V")
             if ok(s):
                 v2(s)

@@ -170,7 +170,7 @@ def tile_feedforward_pa_kernel(
             if q < HEAD_UNITS:
                 return {"V": (0, HEAD_V), "G": (0, 0), "S": (HEAD_V, NT)}
             if through(q):
-                return {"V": (PASS_G, PASS_G + 64), "G": (0, PASS_G), "S": (PASS_G + 64, NT - 2 * P), "T": (NT - 2 * P, NT)}
+                return {"V": (PASS_G, PASS_G + 64), "G": (0, PASS_G), "S": (PASS_G + 64, NT - 1 * P), "T": (NT - 1 * P, NT)}
             return {
                 "V": (0, STEADY_V),
                 "G": (STEADY_V, STEADY_V + STEADY_G),
@@ -203,8 +203,8 @@ def tile_feedforward_pa_kernel(
 
         def pass_pe(q):
             c0 = split(q)["T"][0]
-            pt = psum.tile([P, 2, P, 4], BF16, name="pt", tag="pt", bufs=1)
-            for k in range(2):
+            pt = psum.tile([P, 1, P, 4], BF16, name="pt", tag="pt", bufs=1)
+            for k in range(1):
                 nc.tensor.matmul(
                     out=pt[:, k, :, :],
                     lhsT=ident_b[:],

@@ -37,7 +37,7 @@ G_PRODUCTS = (15, 16, 17, 18)
 
 PASS_FIRST = 10
 PASS_UNITS = 10
-PASS_G = 160
+PASS_G = 128
 SPLIT_FIRST = 4
 SPLIT_PRODUCTS = 10
 HOLD_STORES = 7
@@ -170,7 +170,7 @@ def tile_feedforward_pa_kernel(
             if q < HEAD_UNITS:
                 return {"V": (0, HEAD_V), "G": (0, 0), "S": (HEAD_V, NT)}
             if through(q):
-                return {"V": (PASS_G, PASS_G + 64), "G": (0, PASS_G), "S": (PASS_G + 64, NT - 1 * P), "T": (NT - 1 * P, NT)}
+                return {"V": (PASS_G, PASS_G + 64), "G": (0, PASS_G), "S": (PASS_G + 64, NT - 192), "T": (NT - 192, NT)}
             return {
                 "V": (0, STEADY_V),
                 "G": (STEADY_V, STEADY_V + STEADY_G),
@@ -203,12 +203,12 @@ def tile_feedforward_pa_kernel(
 
         def pass_pe(q):
             c0 = split(q)["T"][0]
-            pt = psum.tile([P, 1, P, 4], BF16, name="pt", tag="pt", bufs=1)
-            for k in range(1):
+            pt = psum.tile([P, 2, 96, 4], BF16, name="pt", tag="pt", bufs=1)
+            for k in range(2):
                 nc.tensor.matmul(
                     out=pt[:, k, :, :],
                     lhsT=ident_b[:],
-                    rhs=raw[q][:, :, c0 + k * P : c0 + (k + 1) * P].rearrange("p t c -> p c t"),
+                    rhs=raw[q][:, :, c0 + k * 96 : c0 + (k + 1) * 96].rearrange("p t c -> p c t"),
                     start=True,
                     stop=True,
                 )

@@ -37,7 +37,8 @@ G_PRODUCTS = (15, 16, 17, 18)
 
 PASS_FIRST = 10
 PASS_UNITS = 10
-PASS_G = 128
+PASS_G = 160
+PASS_V = 0
 SPLIT_FIRST = 4
 SPLIT_PRODUCTS = 10
 HOLD_STORES = 7
@@ -170,7 +171,7 @@ def tile_feedforward_pa_kernel(
             if q < HEAD_UNITS:
                 return {"V": (0, HEAD_V), "G": (0, 0), "S": (HEAD_V, NT)}
             if through(q):
-                return {"V": (PASS_G, PASS_G + 64), "G": (0, PASS_G), "S": (PASS_G + 64, NT - 192), "T": (NT - 192, NT)}
+                return {"V": (PASS_G, PASS_G + PASS_V), "G": (0, PASS_G), "S": (PASS_G + PASS_V, NT - 192), "T": (NT - 192, NT)}
             return {
                 "V": (0, STEADY_V),
                 "G": (STEADY_V, STEADY_V + STEADY_G),

@@ -37,8 +37,9 @@ G_PRODUCTS = (15, 16, 17, 18)
 
 PASS_FIRST = 10
 PASS_UNITS = 10
-PASS_G = 160
+PASS_G = 192
 PASS_V = 0
+PASS_T = 160
 SPLIT_FIRST = 4
 SPLIT_PRODUCTS = 10
 HOLD_STORES = 7
@@ -171,7 +172,7 @@ def tile_feedforward_pa_kernel(
             if q < HEAD_UNITS:
                 return {"V": (0, HEAD_V), "G": (0, 0), "S": (HEAD_V, NT)}
             if through(q):
-                return {"V": (PASS_G, PASS_G + PASS_V), "G": (0, PASS_G), "S": (PASS_G + PASS_V, NT - 192), "T": (NT - 192, NT)}
+                return {"V": (PASS_G, PASS_G + PASS_V), "G": (0, PASS_G), "S": (PASS_G + PASS_V, NT - PASS_T), "T": (NT - PASS_T, NT)}
             return {
                 "V": (0, STEADY_V),
                 "G": (STEADY_V, STEADY_V + STEADY_G),
@@ -204,12 +205,12 @@ def tile_feedforward_pa_kernel(
 
         def pass_pe(q):
             c0 = split(q)["T"][0]
-            pt = psum.tile([P, 2, 96, 4], BF16, name="pt", tag="pt", bufs=1)
+            pt = psum.tile([P, 2, PASS_T // 2, 4], BF16, name="pt", tag="pt", bufs=1)
             for k in range(2):
                 nc.tensor.matmul(
                     out=pt[:, k, :, :],
                     lhsT=ident_b[:],
-                    rhs=raw[q][:, :, c0 + k * 96 : c0 + (k + 1) * 96].rearrange("p t c -> p c t"),
+                    rhs=raw[q][:, :, c0 + k * (PASS_T // 2) : c0 + (k + 1) * (PASS_T // 2)].rearrange("p t c -> p c t"),
                     start=True,
                     stop=True,
                 )

@@ -37,9 +37,9 @@ G_PRODUCTS = (15, 16, 17, 18)
 
 PASS_FIRST = 10
 PASS_UNITS = 10
-PASS_G = 192
+PASS_G = 176
 PASS_V = 0
-PASS_T = 160
+PASS_T = 168
 SPLIT_FIRST = 4
 SPLIT_PRODUCTS = 10
 HOLD_STORES = 7

@@ -83,8 +83,8 @@ def tile_feedforward_pa_kernel(
             bg_sb.append(const.tile([P, NT], BF16, name="bg_sb%d" % j))
             bu_sb.append(const.tile([P, NT], BF16, name="bu_sb%d" % j))
         xg = const.tile([P, TT, NG, P, 4], BF16, name="xg", align_bytes=64)
-        xc = const.tile([P, TT, NG * P], U32, name="xc", align_bytes=64)
-        xs = const.tile([P, TT, NG * P], U8, name="xs", align_bytes=64)
+        xc = const.tile([P, TT, NG * P], U32, name="xc", align_bytes=256)
+        xs = const.tile([P, TT, NG * P], U8, name="xs", align_bytes=256)
         xagT = const.tile([P, TT, P], BF16, name="xagT")
         xauT = const.tile([P, TT, P], BF16, name="xauT")
         s_all = const.tile([P, 8], F32, name="s_all")
@@ -228,8 +228,8 @@ def tile_feedforward_pa_kernel(
         def quantize(q):
             j, u = divmod(q, NU)
             if u == 0:
-                wc[j] = codep.tile([P, NU, NT], U32, name="wc", align_bytes=64)
-                ws[j] = codep.tile([P, NU, NT], U8, name="ws", align_bytes=64)
+                wc[j] = codep.tile([P, NU, NT], U32, name="wc", align_bytes=256)
+                ws[j] = codep.tile([P, NU, NT], U8, name="ws", align_bytes=256)
             nc.vector.quantize_mx(
                 out=wc[j][:, u, :].bitcast(FP8X4),
                 scales=ws[j][:, u, :],

@@ -127,7 +127,7 @@ def tile_feedforward_pa_kernel(
 
         def x_transpose(tt):
             xw = x_sb[tt][:].bitcast(F32)
-            xt = psum.tile([P, NG, 2, P], F32, name="xt", tag=("ug" if tt % 2 == 0 else "uu"))
+            xt = psum.tile([P, NG, 2, P], F32, name="xt", tag=("u" if tt < 2 else "pt"), bufs=(3 if tt < 2 else 1))
             xts[tt] = xt
             for g in range(NG):
                 for u in range(2):
@@ -151,9 +151,9 @@ def tile_feedforward_pa_kernel(
             )
 
         def prep_adapters():
-            pg = psum.tile([P, TT, P], BF16, name="pg", tag="l", bufs=3)
-            pu = psum.tile([P, TT, P], BF16, name="pu", tag="l", bufs=3)
-            pw = psum.tile([P, P], BF16, name="pw", tag="l", bufs=3)
+            pg = psum.tile([P, TT, P], BF16, name="pg", tag="l", bufs=4)
+            pu = psum.tile([P, TT, P], BF16, name="pu", tag="l", bufs=4)
+            pw = psum.tile([P, P], BF16, name="pw", tag="l", bufs=4)
             for tt in range(TT):
                 nc.tensor.transpose(out=pg[:, tt, :], in_=xag[:, tt, :], identity=ident_b[:])
             for tt in range(TT):
@@ -238,16 +238,16 @@ def tile_feedforward_pa_kernel(
 
         def lora_pe(i):
             j, tt = divmod(i, TT)
-            lg = psum.tile([P, NT], F32, name="lg", tag="l", bufs=3)
-            lu = psum.tile([P, NT], F32, name="lu", tag="l", bufs=3)
+            lg = psum.tile([P, NT], F32, name="lg", tag="l", bufs=4)
+            lu = psum.tile([P, NT], F32, name="lu", tag="l", bufs=4)
             nc.tensor.matmul(out=lg[:], lhsT=xagT[:, tt, :], rhs=bg_sb[j][:], start=True, stop=True)
             nc.tensor.matmul(out=lu[:], lhsT=xauT[:, tt, :], rhs=bu_sb[j][:], start=True, stop=True)
             ps_l[i] = (lg, lu)
 
         def mm(i):
             j, tt = divmod(i, TT)
-            ug = psum.tile([P, NT], F32, name="ug", tag="ug")
-            uu = psum.tile([P, NT], F32, name="uu", tag="uu")
+            ug = psum.tile([P, NT], F32, name="ug", tag="u", bufs=3)
+            uu = psum.tile([P, NT], F32, name="uu", tag="u", bufs=3)
             for half, acc in ((0, ug), (1, uu)):
                 for g in range(NG):
                     nc.tensor.matmul_mx(

@@ -31,7 +31,8 @@ HEAD_UNITS = 6
 HEAD_V = 336
 STEADY_V = 0
 STEADY_G = 256
-CAST_V = (512, 512, 1024, 1664)
+CAST_V = (512, 768, 1024, 1792)
+CAST_PIECE = 256
 
 G_PRODUCTS = (15, 16, 17, 18)
 
@@ -41,7 +42,7 @@ PASS_G = 176
 PASS_V = 0
 PASS_T = 168
 SPLIT_FIRST = 4
-SPLIT_PRODUCTS = 10
+SPLIT_PRODUCTS = 11
 HOLD_STORES = 7
 SPLIT_G = 192
 
@@ -288,7 +289,7 @@ def tile_feedforward_pa_kernel(
         def v3(i):
             j, tt = divmod(i, TT)
             hs = h_all[:, tt, j * NT : (j + 1) * NT]
-            if SPLIT_FIRST <= i < SPLIT_FIRST + SPLIT_PRODUCTS:
+            if SPLIT_FIRST <= i < SPLIT_FIRST + SPLIT_PRODUCTS or i == NTILE - 1:
                 cv = NT - SPLIT_G
                 nc.vector.tensor_tensor(
                     out=hs[:, 0:cv], in0=sb[i]["up"][:, 0:cv], in1=sb[i]["sg"][:, 0:cv], op=ALU.mult
@@ -341,12 +342,12 @@ def tile_feedforward_pa_kernel(
         def cast_cols(tt):
             return CAST_V[tt]
 
-        def cast_v(tt):
-            cv = cast_cols(tt)
-            o8[tt] = o8p.tile([P, HID], FP8, name="o8")
+        def cast_v(tt, c0, c1):
+            if tt not in o8:
+                o8[tt] = o8p.tile([P, HID], FP8, name="o8")
             nc.vector.tensor_scalar(
-                out=o8[tt][:, 0:cv],
-                in0=h_all[:, tt, 0:cv],
+                out=o8[tt][:, c0:c1],
+                in0=h_all[:, tt, c0:c1],
                 scalar1=rsc[:, tt : tt + 1],
                 scalar2=None,
                 op0=ALU.mult,
@@ -363,6 +364,8 @@ def tile_feedforward_pa_kernel(
                 bias=zeros[:, 0:1],
                 saturate=False,
             )
+
+        def store8(tt):
             nc.sync.dma_start(out=o1[tt * P : (tt + 1) * P, :], in_=o8[tt][:].bitcast(U8))
 
         nc.vector.memset(zeros[:], 0.0)
@@ -477,22 +480,32 @@ def tile_feedforward_pa_kernel(
                 v2(s)
             if last(s - 2):
                 fin_c((s - 2) % TT)
+            if s - 2 == NTILE - 1:
+                cast_v(TT - 2, 3 * CAST_PIECE, cast_cols(TT - 2))
+                store8(TT - 2)
             if ok(s + 2):
                 s12(s + 2)
             if s <= 1:
                 x_copy(s + 2)
             if ok(s - 1):
                 v4(s - 1)
-            if last(s - 2):
-                cast_v((s - 2) % TT)
-                cast_s((s - 2) % TT)
             if ok(s + 1):
                 v1(s + 1)
+            woven = s - 2 == NTILE - 2
+            if last(s - 2):
+                cast_v((s - 2) % TT, 0, CAST_PIECE if woven else cast_cols((s - 2) % TT))
+                cast_s((s - 2) % TT)
+                if not woven:
+                    store8((s - 2) % TT)
             if last(s - 1):
                 fin_a((s - 1) % TT)
+            if woven:
+                cast_v(TT - 2, CAST_PIECE, 2 * CAST_PIECE)
             if qi < NUNIT:
                 next_load(qi)
             if ok(s) and not late(s):
                 v3(s)
             if last(s - 1):
                 fin_b((s - 1) % TT)
+            if woven:
+                cast_v(TT - 2, 2 * CAST_PIECE, 3 * CAST_PIECE)

@@ -441,29 +441,31 @@ def tile_feedforward_pa_kernel(
         quantize(3)
         quant_x(1)
         mm(0)
+        x_transpose(2)
         lora_pe(2)
         interleave(4, "V")
         interleave(4, "G")
         interleave(4, "S")
         next_load(4)
+        x_copy(2)
         v1(0)
         for s in range(0, NTILE + 3):
             qq = s + 4
             qi = s + 5
-            if 1 <= s <= 2:
-                quant_x(s + 1)
             if qi < NUNIT and through(qi):
                 interleave(qi, "V")
             if qq < NUNIT:
                 quantize(qq)
+            if s <= 1:
+                quant_x(s + 2)
             if qi < NUNIT:
                 interleave(qi, "G")
             if ok(s - 1) and late(s - 1):
                 v3(s - 1)
             if ok(s + 1):
                 mm(s + 1)
-            if s <= 1:
-                x_transpose(s + 2)
+            if s == 0:
+                x_transpose(3)
             if qi < NUNIT:
                 if through(qi):
                     pass_s(qi)
@@ -485,12 +487,12 @@ def tile_feedforward_pa_kernel(
                 store8(TT - 2)
             if ok(s + 2):
                 s12(s + 2)
-            if s <= 1:
-                x_copy(s + 2)
-            if ok(s - 1):
-                v4(s - 1)
+            if s == 0:
+                x_copy(3)
             if ok(s + 1):
                 v1(s + 1)
+            if ok(s - 1):
+                v4(s - 1)
             woven = s - 2 == NTILE - 2
             if last(s - 2):
                 cast_v((s - 2) % TT, 0, CAST_PIECE if woven else cast_cols((s - 2) % TT))

@@ -419,10 +419,10 @@ def tile_feedforward_pa_kernel(
         x_transpose(0)
         x_copy(0)
         quantize(0)
-        quant_x(0)
         interleave(1, "V")
         interleave(1, "S")
         next_load(1)
+        quant_x(0)
         prep_adapters()
         quantize(1)
         interleave(2, "V")
@@ -434,12 +434,11 @@ def tile_feedforward_pa_kernel(
         interleave(3, "V")
         interleave(3, "S")
         next_load(3)
-        x_transpose(1)
-        x_copy(1)
         lora_pe(1)
         s12(1)
+        x_transpose(1)
+        x_copy(1)
         quantize(3)
-        quant_x(1)
         mm(0)
         x_transpose(2)
         lora_pe(2)
@@ -447,6 +446,7 @@ def tile_feedforward_pa_kernel(
         interleave(4, "G")
         interleave(4, "S")
         next_load(4)
+        quant_x(1)
         x_copy(2)
         v1(0)
         for s in range(0, NTILE + 3):

@@ -392,8 +392,8 @@ def tile_feedforward_pa_kernel(
         load_unit(4)
         load_x(2)
         load_unit(5)
-        load_x(3)
         load_unit(6)
+        load_x(3)
         load_b(nc.sync, 1)
         load_unit(7)
 

@@ -72,7 +72,8 @@ def tile_feedforward_pa_kernel(
         junk = const.tile([P, 1], F32, name="junk")
         ident_f = const.tile([P, P], F32, name="ident_f")
         ident_b = const.tile([P, P], BF16, name="ident_b")
-        twr = const.tile([P, P], BF16, name="twr")
+        twu = const.tile([P, TT], BF16, name="twu")
+        twg = const.tile([P, TT], BF16, name="twg")
         xag = const.tile([P, TT, RANK], BF16, name="xag")
         xau = const.tile([P, TT, RANK], BF16, name="xau")
         x_sb = []
@@ -105,7 +106,7 @@ def tile_feedforward_pa_kernel(
         o8 = {}
 
         def load_x(tt):
-            nc.sync.dma_start(out=x_sb[tt][:], in_=xf[tt * P : (tt + 1) * P, :])
+            nc.sync.dma_start(out=x_sb[tt][:], in_=xf[tt:TOK:TT, :])
 
         def load_unit(q):
             j, u = divmod(q, NU)
@@ -154,16 +155,17 @@ def tile_feedforward_pa_kernel(
         def prep_adapters():
             pg = psum.tile([P, TT, P], BF16, name="pg", tag="l", bufs=4)
             pu = psum.tile([P, TT, P], BF16, name="pu", tag="l", bufs=4)
-            pw = psum.tile([P, P], BF16, name="pw", tag="l", bufs=4)
             for tt in range(TT):
                 nc.tensor.transpose(out=pg[:, tt, :], in_=xag[:, tt, :], identity=ident_b[:])
             for tt in range(TT):
                 nc.tensor.transpose(out=pu[:, tt, :], in_=xau[:, tt, :], identity=ident_b[:])
-            nc.tensor.transpose(out=pw[:], in_=twr[:], identity=ident_b[:])
             nc.scalar.copy(out=xagT[:], in_=pg[:])
             nc.scalar.copy(out=xauT[:], in_=pu[:])
             nc.vector.tensor_scalar(
-                out=s_all[:], in0=pw[:, 0:8], scalar1=4.0, scalar2=None, op0=ALU.mult
+                out=s_all[:, 0:TT], in0=twu[:], scalar1=4.0, scalar2=None, op0=ALU.mult
+            )
+            nc.vector.tensor_scalar(
+                out=s_all[:, TT : 2 * TT], in0=twg[:], scalar1=4.0, scalar2=None, op0=ALU.mult
             )
 
         def through(q):
@@ -308,7 +310,7 @@ def tile_feedforward_pa_kernel(
         def store(i):
             j, tt = divmod(i, TT)
             nc.sync.dma_start(
-                out=o0[tt * P : (tt + 1) * P, j * NT : (j + 1) * NT],
+                out=o0[tt:TOK:TT, j * NT : (j + 1) * NT],
                 in_=h_all[:, tt, j * NT : (j + 1) * NT],
             )
 
@@ -366,10 +368,9 @@ def tile_feedforward_pa_kernel(
             )
 
         def store8(tt):
-            nc.sync.dma_start(out=o1[tt * P : (tt + 1) * P, :], in_=o8[tt][:].bitcast(U8))
+            nc.sync.dma_start(out=o1[tt:TOK:TT, :], in_=o8[tt][:].bitcast(U8))
 
         nc.vector.memset(zeros[:], 0.0)
-        nc.gpsimd.memset(twr[:], 0.0)
         nc.scalar.activation(out=junk[:], in_=zeros[:], func=ACT.Silu)
         make_identity(nc, ident_f[:])
         make_identity(nc, ident_b[:])
@@ -378,13 +379,13 @@ def tile_feedforward_pa_kernel(
         load_x(0)
         load_unit(1)
         nc.sync.dma_start(
-            out=xag[:], in_=xa_gate.flatten_outer_dims().rearrange("(t p) r -> p t r", p=P)
+            out=xag[:], in_=xa_gate.flatten_outer_dims().rearrange("(p t) r -> p t r", t=TT)
         )
         nc.sync.dma_start(
-            out=xau[:], in_=xa_up.flatten_outer_dims().rearrange("(t p) r -> p t r", p=P)
+            out=xau[:], in_=xa_up.flatten_outer_dims().rearrange("(p t) r -> p t r", t=TT)
         )
-        nc.sync.dma_start(out=twr[0:4, :], in_=tw_up.rearrange("(t h) s -> t (h s)", h=2))
-        nc.sync.dma_start(out=twr[4:8, :], in_=tw_gate.rearrange("(t h) s -> t (h s)", h=2))
+        nc.sync.dma_start(out=twu[:], in_=tw_up.rearrange("b (m t) -> (b m) t", t=TT))
+        nc.sync.dma_start(out=twg[:], in_=tw_gate.rearrange("b (m t) -> (b m) t", t=TT))
         load_unit(2)
         load_b(nc.sync, 0)
         load_unit(3)

@@ -455,13 +455,15 @@ def tile_feedforward_pa_kernel(
             qi = s + 5
             if qi < NUNIT and through(qi):
                 interleave(qi, "V")
+            if s == 1:
+                v3(0)
             if qq < NUNIT:
                 quantize(qq)
             if s <= 1:
                 quant_x(s + 2)
             if qi < NUNIT:
                 interleave(qi, "G")
-            if ok(s - 1) and late(s - 1):
+            if ok(s - 1) and late(s - 1) and s != 1:
                 v3(s - 1)
             if ok(s + 1):
                 mm(s + 1)

@@ -265,17 +265,24 @@ def tile_feedforward_pa_kernel(
             ps_u[i] = (ug, uu)
 
         def s12(i):
-            tt = i % TT
             lg, lu = ps_l[i]
             ag = lorap.tile([P, NT], F32, name="ag")
             au = lorap.tile([P, NT], F32, name="au")
-            nc.scalar.activation(out=ag[:], in_=lg[:], func=ACT.Copy, scale=s_all[:, 4 + tt : 5 + tt])
-            nc.scalar.activation(out=au[:], in_=lu[:], func=ACT.Copy, scale=s_all[:, tt : tt + 1])
+            nc.scalar.copy(out=ag[:], in_=lg[:])
+            nc.scalar.copy(out=au[:], in_=lu[:])
             sb[i] = {"ag": ag, "au": au}
 
         def v1(i):
             gt = epi.tile([P, NT], F32, name="gt")
-            nc.vector.tensor_tensor(out=gt[:], in0=ps_u[i][0][:], in1=sb[i]["ag"][:], op=ALU.add)
+            tt = i % TT
+            nc.vector.scalar_tensor_tensor(
+                out=gt[:],
+                in0=sb[i]["ag"][:],
+                scalar=s_all[:, 4 + tt : 5 + tt],
+                in1=ps_u[i][0][:],
+                op0=ALU.mult,
+                op1=ALU.add,
+            )
             sb[i]["gt"] = gt
 
         def s3(i):
@@ -285,7 +292,15 @@ def tile_feedforward_pa_kernel(
 
         def v2(i):
             up = epi.tile([P, NT], F32, name="up")
-            nc.vector.tensor_tensor(out=up[:], in0=ps_u[i][1][:], in1=sb[i]["au"][:], op=ALU.add)
+            tt = i % TT
+            nc.vector.scalar_tensor_tensor(
+                out=up[:],
+                in0=sb[i]["au"][:],
+                scalar=s_all[:, tt : tt + 1],
+                in1=ps_u[i][1][:],
+                op0=ALU.mult,
+                op1=ALU.add,
+            )
             sb[i]["up"] = up
 
         def v3(i):

@@ -40,7 +40,7 @@ PASS_FIRST = 10
 PASS_UNITS = 10
 PASS_G = 176
 PASS_V = 0
-PASS_T = 168
+PASS_T = 248
 SPLIT_FIRST = 4
 SPLIT_PRODUCTS = 11
 HOLD_STORES = 7
@@ -211,9 +211,9 @@ def tile_feedforward_pa_kernel(
             pt = psum.tile([P, 2, PASS_T // 2, 4], BF16, name="pt", tag="pt", bufs=1)
             for k in range(2):
                 nc.tensor.matmul(
-                    out=pt[:, k, :, :],
+                    out=pt[:, k, :, :].rearrange("p (c i) t -> p c t i", i=4),
                     lhsT=ident_b[:],
-                    rhs=raw[q][:, :, c0 + k * (PASS_T // 2) : c0 + (k + 1) * (PASS_T // 2)].rearrange("p t c -> p c t"),
+                    rhs=raw[q][:, :, c0 + k * (PASS_T // 2) : c0 + (k + 1) * (PASS_T // 2)].rearrange("p t (c i) -> p c t i", i=4),
                     start=True,
                     stop=True,
                 )

@@ -38,13 +38,13 @@ G_PRODUCTS = (15, 16, 17, 18)
 
 PASS_FIRST = 10
 PASS_UNITS = 10
-PASS_G = 176
+PASS_G = 160
 PASS_V = 0
-PASS_T = 248
+PASS_T = 200
 SPLIT_FIRST = 4
 SPLIT_PRODUCTS = 11
 HOLD_STORES = 7
-SPLIT_G = 192
+SPLIT_G = 256
 
 FLOPS = 2 * TOK * DIM * HID * 2 + 2 * TOK * RANK * HID * 2
 

@@ -36,13 +36,13 @@ CAST_PIECE = 256
 
 G_PRODUCTS = (15, 16, 17, 18)
 
-PASS_FIRST = 10
-PASS_UNITS = 10
+PASS_FIRST = 8
+PASS_UNITS = 12
 PASS_G = 160
 PASS_V = 0
 PASS_T = 200
-SPLIT_FIRST = 4
-SPLIT_PRODUCTS = 11
+SPLIT_FIRST = 2
+SPLIT_PRODUCTS = 13
 HOLD_STORES = 7
 SPLIT_G = 256
 

@@ -90,8 +90,7 @@ def tile_feedforward_pa_kernel(
         xagT = const.tile([P, TT, P], BF16, name="xagT")
         xauT = const.tile([P, TT, P], BF16, name="xauT")
         s_all = const.tile([P, 8], F32, name="s_all")
-        h_all = const.tile([P, TT, HID], F32, name="h_all")
-        stats = const.tile([P, TT, 8], F32, name="stats")
+        h_all = const.tile([P, TT, HID + 8], F32, name="h_all")
         amax = const.tile([P, TT], F32, name="amax")
         rcp = const.tile([P, TT], F32, name="rcp")
         rsc = const.tile([P, TT], F32, name="rsc")
@@ -306,7 +305,7 @@ def tile_feedforward_pa_kernel(
         def v3(i):
             j, tt = divmod(i, TT)
             hs = h_all[:, tt, j * NT : (j + 1) * NT]
-            if SPLIT_FIRST <= i < SPLIT_FIRST + SPLIT_PRODUCTS or i == NTILE - 1:
+            if SPLIT_FIRST <= i < SPLIT_FIRST + SPLIT_PRODUCTS:
                 cv = NT - SPLIT_G
                 nc.vector.tensor_tensor(
                     out=hs[:, 0:cv], in0=sb[i]["up"][:, 0:cv], in1=sb[i]["sg"][:, 0:cv], op=ALU.mult
@@ -331,18 +330,22 @@ def tile_feedforward_pa_kernel(
 
         def v4(i):
             j, tt = divmod(i, TT)
-            nc.vector.tensor_reduce(
-                out=stats[:, tt, j : j + 1],
-                in_=h_all[:, tt, j * NT : (j + 1) * NT],
-                axis=AX.X,
-                op=ALU.max,
-                apply_absolute_value=True,
-            )
-
-        def fin_a(tt):
-            nc.vector.tensor_reduce(
-                out=amax[:, tt : tt + 1], in_=stats[:, tt, 0:NJ], axis=AX.X, op=ALU.max
-            )
+            if j < NJ - 1:
+                nc.vector.tensor_reduce(
+                    out=h_all[:, tt, HID + j : HID + j + 1],
+                    in_=h_all[:, tt, j * NT : (j + 1) * NT],
+                    axis=AX.X,
+                    op=ALU.max,
+                    apply_absolute_value=True,
+                )
+            else:
+                nc.vector.tensor_reduce(
+                    out=amax[:, tt : tt + 1],
+                    in_=h_all[:, tt, j * NT : HID + NJ - 1],
+                    axis=AX.X,
+                    op=ALU.max,
+                    apply_absolute_value=True,
+                )
 
         def fin_b(tt):
             nc.vector.reciprocal(out=rcp[:, tt : tt + 1], in_=amax[:, tt : tt + 1])
@@ -498,8 +501,6 @@ def tile_feedforward_pa_kernel(
                 interleave(qi, "V")
             if ok(s):
                 v2(s)
-            if last(s - 2):
-                fin_c((s - 2) % TT)
             if s - 2 == NTILE - 1:
                 cast_v(TT - 2, 3 * CAST_PIECE, cast_cols(TT - 2))
                 store8(TT - 2)
@@ -518,7 +519,7 @@ def tile_feedforward_pa_kernel(
                 if not woven:
                     store8((s - 2) % TT)
             if last(s - 1):
-                fin_a((s - 1) % TT)
+                fin_b((s - 1) % TT)
             if woven:
                 cast_v(TT - 2, CAST_PIECE, 2 * CAST_PIECE)
             if qi < NUNIT:
@@ -526,6 +527,6 @@ def tile_feedforward_pa_kernel(
             if ok(s) and not late(s):
                 v3(s)
             if last(s - 1):
-                fin_b((s - 1) % TT)
+                fin_c((s - 1) % TT)
             if woven:
                 cast_v(TT - 2, 2 * CAST_PIECE, 3 * CAST_PIECE)

@@ -513,10 +513,14 @@ def tile_feedforward_pa_kernel(
             if ok(s - 1):
                 v4(s - 1)
             woven = s - 2 == NTILE - 2
+            held = s - 2 == NTILE - TT
             if last(s - 2):
-                cast_v((s - 2) % TT, 0, CAST_PIECE if woven else cast_cols((s - 2) % TT))
+                if not held:
+                    cast_v((s - 2) % TT, 0, CAST_PIECE if woven else cast_cols((s - 2) % TT))
+                else:
+                    o8[0] = o8p.tile([P, HID], FP8, name="o8")
                 cast_s((s - 2) % TT)
-                if not woven:
+                if not woven and not held:
                     store8((s - 2) % TT)
             if last(s - 1):
                 fin_b((s - 1) % TT)
@@ -528,5 +532,8 @@ def tile_feedforward_pa_kernel(
                 v3(s)
             if last(s - 1):
                 fin_c((s - 1) % TT)
+            if held:
+                cast_v(0, 0, cast_cols(0))
+                store8(0)
             if woven:
                 cast_v(TT - 2, 2 * CAST_PIECE, 3 * CAST_PIECE)

@@ -40,7 +40,7 @@ PASS_FIRST = 8
 PASS_UNITS = 12
 PASS_G = 160
 PASS_V = 0
-PASS_T = 200
+PASS_T = 224
 SPLIT_FIRST = 2
 SPLIT_PRODUCTS = 13
 HOLD_STORES = 7

@@ -388,6 +388,8 @@ def tile_feedforward_pa_kernel(
         def store8(tt):
             nc.sync.dma_start(out=o1[tt:TOK:TT, :], in_=o8[tt][:].bitcast(U8))
 
+        nc.scalar.dma_start(out=twu[:], in_=tw_up.rearrange("b (m t) -> (b m) t", t=TT))
+        nc.scalar.dma_start(out=twg[:], in_=tw_gate.rearrange("b (m t) -> (b m) t", t=TT))
         nc.vector.memset(zeros[:], 0.0)
         nc.scalar.activation(out=junk[:], in_=zeros[:], func=ACT.Silu)
         make_identity(nc, ident_f[:])
@@ -402,8 +404,6 @@ def tile_feedforward_pa_kernel(
         nc.sync.dma_start(
             out=xau[:], in_=xa_up.flatten_outer_dims().rearrange("(p t) r -> p t r", t=TT)
         )
-        nc.sync.dma_start(out=twu[:], in_=tw_up.rearrange("b (m t) -> (b m) t", t=TT))
-        nc.sync.dma_start(out=twg[:], in_=tw_gate.rearrange("b (m t) -> (b m) t", t=TT))
         load_unit(2)
         load_b(nc.sync, 0)
         load_unit(3)

from contextlib import ExitStack

import concourse.mybir as mybir
from concourse.masks import make_identity

F32 = mybir.dt.float32
BF16 = mybir.dt.bfloat16
U32 = mybir.dt.uint32
U8 = mybir.dt.uint8
FP8X4 = mybir.dt.float8_e4m3fn_x4
FP8 = mybir.dt.float8_e4m3fn
ACT = mybir.ActivationFunctionType
ALU = mybir.AluOpType
AX = mybir.AxisListType

P = 128
TOK = 512
DIM = 1024
HID = 2560
RANK = 128
TT = TOK // P
NT = 512
NJ = HID // NT
NG = DIM // 512
NU = 2 * NG
NTILE = NJ * TT
NUNIT = NJ * NU
RAW_BUFS = 8
GRP_BUFS = 2
HEAD_UNITS = 6
HEAD_V = 336
STEADY_V = 0
STEADY_G = 256
CAST_V = (512, 768, 1024, 1792)
CAST_PIECE = 256

G_PRODUCTS = (15, 16, 17, 18)

PASS_FIRST = 8
PASS_UNITS = 12
PASS_G = 160
PASS_V = 0
PASS_T = 224
SPLIT_FIRST = 2
SPLIT_PRODUCTS = 13
HOLD_STORES = 7
SPLIT_G = 256

FLOPS = 2 * TOK * DIM * HID * 2 + 2 * TOK * RANK * HID * 2


def tile_feedforward_pa_kernel(
    tc, x, w1, w3, xa_up, b_up, xa_gate, b_gate, tw_up, tw_gate, out_0, out_1
):
    nc = tc.nc
    xf = x.flatten_outer_dims()
    o0 = out_0.flatten_outer_dims()
    o1 = out_1.flatten_outer_dims()

    with ExitStack() as ctx:
        const = ctx.enter_context(tc.tile_pool(name="const", bufs=1))
        rawp = ctx.enter_context(tc.tile_pool(name="rawp", bufs=RAW_BUFS))
        grpp = ctx.enter_context(tc.tile_pool(name="grpp", bufs=GRP_BUFS))
        codep = ctx.enter_context(tc.tile_pool(name="codep", bufs=3))
        lorap = ctx.enter_context(tc.tile_pool(name="lorap", bufs=4))
        epi = ctx.enter_context(tc.tile_pool(name="epi", bufs=3))
        o8p = ctx.enter_context(tc.tile_pool(name="o8p", bufs=4))
        psum = ctx.enter_context(tc.psum_pool(name="psum", bufs=2))
        ctx.enter_context(tc.manual_schedule())

        zeros = const.tile([P, 1], F32, name="zeros")
        junk = const.tile([P, 1], F32, name="junk")
        ident_f = const.tile([P, P], F32, name="ident_f")
        ident_b = const.tile([P, P], BF16, name="ident_b")
        twu = const.tile([P, TT], BF16, name="twu")
        twg = const.tile([P, TT], BF16, name="twg")
        xag = const.tile([P, TT, RANK], BF16, name="xag")
        xau = const.tile([P, TT, RANK], BF16, name="xau")
        x_sb = []
        for tt in range(TT):
            x_sb.append(const.tile([P, DIM], BF16, name="x_sb%d" % tt))
        bg_sb = []
        bu_sb = []
        for j in range(NJ):
            bg_sb.append(const.tile([P, NT], BF16, name="bg_sb%d" % j))
            bu_sb.append(const.tile([P, NT], BF16, name="bu_sb%d" % j))
        xg = const.tile([P, TT, NG, P, 4], BF16, name="xg", align_bytes=64)
        xc = const.tile([P, TT, NG * P], U32, name="xc", align_bytes=256)
        xs = const.tile([P, TT, NG * P], U8, name="xs", align_bytes=256)
        xagT = const.tile([P, TT, P], BF16, name="xagT")
        xauT = const.tile([P, TT, P], BF16, name="xauT")
        s_all = const.tile([P, 8], F32, name="s_all")
        h_all = const.tile([P, TT, HID + 8], F32, name="h_all")
        amax = const.tile([P, TT], F32, name="amax")
        rcp = const.tile([P, TT], F32, name="rcp")
        rsc = const.tile([P, TT], F32, name="rsc")

        raw = {}
        grp = {}
        wc = {}
        ws = {}
        ps_l = {}
        ps_u = {}
        sb = {}
        o8 = {}

        def load_x(tt):
            nc.sync.dma_start(out=x_sb[tt][:], in_=xf[tt:TOK:TT, :])

        def load_unit(q):
            j, u = divmod(q, NU)
            w = w1 if u < NG else w3
            g = u % NG
            t = rawp.tile([P, 4, NT], BF16, name="raw")
            nc.sync.dma_start(
                out=t[:],
                in_=w[g * 512 : (g + 1) * 512, j * NT : (j + 1) * NT].rearrange(
                    "(p t) c -> p t c", t=4
                ),
            )
            raw[q] = t

        def load_b(eng, j):
            eng.dma_start(out=bg_sb[j][:], in_=b_gate[:, j * NT : (j + 1) * NT])
            eng.dma_start(out=bu_sb[j][:], in_=b_up[:, j * NT : (j + 1) * NT])

        xts = {}

        def x_transpose(tt):
            xw = x_sb[tt][:].bitcast(F32)
            xt = psum.tile([P, NG, 2, P], F32, name="xt", tag=("u" if tt < 2 else "pt"), bufs=(3 if tt < 2 else 1))
            xts[tt] = xt
            for g in range(NG):
                for u in range(2):
                    nc.tensor.transpose(
                        out=xt[:, g, u, :],
                        in_=xw[:, 256 * g + u : 256 * (g + 1) : 2],
                        identity=ident_f[:],
                    )

        def x_copy(tt):
            nc.scalar.copy(
                out=xg[:, tt, :, :, :].bitcast(F32),
                in_=xts[tt][:].rearrange("p g u r -> p g r u"),
            )

        def quant_x(tt):
            nc.vector.quantize_mx(
                out=xc[:, tt, :].bitcast(FP8X4),
                scales=xs[:, tt, :],
                in_=xg[:, tt, :, :, :].rearrange("p g r t -> p (g r t)"),
            )

        def prep_adapters():
            pg = psum.tile([P, TT, P], BF16, name="pg", tag="l", bufs=4)
            pu = psum.tile([P, TT, P], BF16, name="pu", tag="l", bufs=4)
            for tt in range(TT):
                nc.tensor.transpose(out=pg[:, tt, :], in_=xag[:, tt, :], identity=ident_b[:])
            for tt in range(TT):
                nc.tensor.transpose(out=pu[:, tt, :], in_=xau[:, tt, :], identity=ident_b[:])
            nc.scalar.copy(out=xagT[:], in_=pg[:])
            nc.scalar.copy(out=xauT[:], in_=pu[:])
            nc.vector.tensor_scalar(
                out=s_all[:, 0:TT], in0=twu[:], scalar1=4.0, scalar2=None, op0=ALU.mult
            )
            nc.vector.tensor_scalar(
                out=s_all[:, TT : 2 * TT], in0=twg[:], scalar1=4.0, scalar2=None, op0=ALU.mult
            )

        def through(q):
            return PASS_FIRST <= q < PASS_FIRST + PASS_UNITS

        def split(q):
            if q < HEAD_UNITS:
                return {"V": (0, HEAD_V), "G": (0, 0), "S": (HEAD_V, NT)}
            if through(q):
                return {"V": (PASS_G, PASS_G + PASS_V), "G": (0, PASS_G), "S": (PASS_G + PASS_V, NT - PASS_T), "T": (NT - PASS_T, NT)}
            return {
                "V": (0, STEADY_V),
                "G": (STEADY_V, STEADY_V + STEADY_G),
                "S": (STEADY_V + STEADY_G, NT),
            }

        def interleave(q, who):
            if q not in grp:
                grp[q] = grpp.tile([P, NT, 4], BF16, name="grp", align_bytes=64)
            c0, c1 = split(q)[who]
            if c1 <= c0:
                return
            src = raw[q][:, :, c0:c1].rearrange("p t (c i) -> p c t i", i=4)
            dst = grp[q][:, c0:c1, :].rearrange("p (c i) t -> p c t i", i=4)
            if who == "V":
                nc.vector.tensor_copy(out=dst, in_=src)
            elif who == "S":
                nc.scalar.copy(out=dst, in_=src)
            else:
                nc.gpsimd.tensor_scalar(
                    out=grp[q][:, c0:c1, :],
                    in0=raw[q][:, :, c0:c1].rearrange("p t c -> p c t"),
                    scalar1=1.0,
                    scalar2=0.0,
                    op0=ALU.mult,
                    op1=ALU.add,
                )

        pts = {}

        def pass_pe(q):
            c0 = split(q)["T"][0]
            pt = psum.tile([P, 2, PASS_T // 2, 4], BF16, name="pt", tag="pt", bufs=1)
            for k in range(2):
                nc.tensor.matmul(
                    out=pt[:, k, :, :].rearrange("p (c i) t -> p c t i", i=4),
                    lhsT=ident_b[:],
                    rhs=raw[q][:, :, c0 + k * (PASS_T // 2) : c0 + (k + 1) * (PASS_T // 2)].rearrange("p t (c i) -> p c t i", i=4),
                    start=True,
                    stop=True,
                )
            pts[q] = pt

        def pass_s(q):
            if q not in grp:
                grp[q] = grpp.tile([P, NT, 4], BF16, name="grp", align_bytes=64)
            c0, c1 = split(q)["T"]
            nc.scalar.copy(
                out=grp[q][:, c0:c1, :].rearrange("p c t -> p (c t)"),
                in_=pts[q][:].rearrange("p k c t -> p (k c t)"),
            )

        def quantize(q):
            j, u = divmod(q, NU)
            if u == 0:
                wc[j] = codep.tile([P, NU, NT], U32, name="wc", align_bytes=256)
                ws[j] = codep.tile([P, NU, NT], U8, name="ws", align_bytes=256)
            nc.vector.quantize_mx(
                out=wc[j][:, u, :].bitcast(FP8X4),
                scales=ws[j][:, u, :],
                in_=grp[q][:].rearrange("p c t -> p (c t)"),
            )

        def lora_pe(i):
            j, tt = divmod(i, TT)
            lg = psum.tile([P, NT], F32, name="lg", tag="l", bufs=4)
            lu = psum.tile([P, NT], F32, name="lu", tag="l", bufs=4)
            nc.tensor.matmul(out=lg[:], lhsT=xagT[:, tt, :], rhs=bg_sb[j][:], start=True, stop=True)
            nc.tensor.matmul(out=lu[:], lhsT=xauT[:, tt, :], rhs=bu_sb[j][:], start=True, stop=True)
            ps_l[i] = (lg, lu)

        def mm(i):
            j, tt = divmod(i, TT)
            ug = psum.tile([P, NT], F32, name="ug", tag="u", bufs=3)
            uu = psum.tile([P, NT], F32, name="uu", tag="u", bufs=3)
            for half, acc in ((0, ug), (1, uu)):
                for g in range(NG):
                    nc.tensor.matmul_mx(
                        out=acc[:],
                        lhsT=xc[:, tt, g * P : (g + 1) * P].bitcast(FP8X4),
                        lhsT_scale=xs[:, tt, g * P : (g + 1) * P],
                        rhs=wc[j][:, half * NG + g, :].bitcast(FP8X4),
                        rhs_scale=ws[j][:, half * NG + g, :],
                        start=(g == 0),
                        stop=(g == NG - 1),
                    )
            ps_u[i] = (ug, uu)

        def s12(i):
            lg, lu = ps_l[i]
            ag = lorap.tile([P, NT], F32, name="ag")
            au = lorap.tile([P, NT], F32, name="au")
            nc.scalar.copy(out=ag[:], in_=lg[:])
            nc.scalar.copy(out=au[:], in_=lu[:])
            sb[i] = {"ag": ag, "au": au}

        def v1(i):
            gt = epi.tile([P, NT], F32, name="gt")
            tt = i % TT
            nc.vector.scalar_tensor_tensor(
                out=gt[:],
                in0=sb[i]["ag"][:],
                scalar=s_all[:, 4 + tt : 5 + tt],
                in1=ps_u[i][0][:],
                op0=ALU.mult,
                op1=ALU.add,
            )
            sb[i]["gt"] = gt

        def s3(i):
            sg = epi.tile([P, NT], F32, name="sg")
            nc.scalar.activation(out=sg[:], in_=sb[i]["gt"][:], func=ACT.Silu)
            sb[i]["sg"] = sg

        def v2(i):
            up = epi.tile([P, NT], F32, name="up")
            tt = i % TT
            nc.vector.scalar_tensor_tensor(
                out=up[:],
                in0=sb[i]["au"][:],
                scalar=s_all[:, tt : tt + 1],
                in1=ps_u[i][1][:],
                op0=ALU.mult,
                op1=ALU.add,
            )
            sb[i]["up"] = up

        def v3(i):
            j, tt = divmod(i, TT)
            hs = h_all[:, tt, j * NT : (j + 1) * NT]
            if SPLIT_FIRST <= i < SPLIT_FIRST + SPLIT_PRODUCTS:
                cv = NT - SPLIT_G
                nc.vector.tensor_tensor(
                    out=hs[:, 0:cv], in0=sb[i]["up"][:, 0:cv], in1=sb[i]["sg"][:, 0:cv], op=ALU.mult
                )
                nc.gpsimd.tensor_tensor(
                    out=hs[:, cv:NT], in0=sb[i]["up"][:, cv:NT], in1=sb[i]["sg"][:, cv:NT], op=ALU.mult
                )
            else:
                eng = nc.gpsimd if i in G_PRODUCTS else nc.vector
                eng.tensor_tensor(out=hs, in0=sb[i]["up"][:], in1=sb[i]["sg"][:], op=ALU.mult)
            if i + 1 >= HOLD_STORES:
                store(i)
                if i + 1 - HOLD_STORES < HOLD_STORES - 1:
                    store(i + 1 - HOLD_STORES)

        def store(i):
            j, tt = divmod(i, TT)
            nc.sync.dma_start(
                out=o0[tt:TOK:TT, j * NT : (j + 1) * NT],
                in_=h_all[:, tt, j * NT : (j + 1) * NT],
            )

        def v4(i):
            j, tt = divmod(i, TT)
            if j < NJ - 1:
                nc.vector.tensor_reduce(
                    out=h_all[:, tt, HID + j : HID + j + 1],
                    in_=h_all[:, tt, j * NT : (j + 1) * NT],
                    axis=AX.X,
                    op=ALU.max,
                    apply_absolute_value=True,
                )
            else:
                nc.vector.tensor_reduce(
                    out=amax[:, tt : tt + 1],
                    in_=h_all[:, tt, j * NT : HID + NJ - 1],
                    axis=AX.X,
                    op=ALU.max,
                    apply_absolute_value=True,
                )

        def fin_b(tt):
            nc.vector.reciprocal(out=rcp[:, tt : tt + 1], in_=amax[:, tt : tt + 1])

        def fin_c(tt):
            nc.vector.tensor_scalar(
                out=rsc[:, tt : tt + 1],
                in0=rcp[:, tt : tt + 1],
                scalar1=448.0,
                scalar2=None,
                op0=ALU.mult,
            )

        def cast_cols(tt):
            return CAST_V[tt]

        def cast_v(tt, c0, c1):
            if tt not in o8:
                o8[tt] = o8p.tile([P, HID], FP8, name="o8")
            nc.vector.tensor_scalar(
                out=o8[tt][:, c0:c1],
                in0=h_all[:, tt, c0:c1],
                scalar1=rsc[:, tt : tt + 1],
                scalar2=None,
                op0=ALU.mult,
                saturate=False,
            )

        def cast_s(tt):
            cv = cast_cols(tt)
            nc.scalar.activation(
                out=o8[tt][:, cv:HID],
                in_=h_all[:, tt, cv:HID],
                func=ACT.Identity,
                scale=rsc[:, tt : tt + 1],
                bias=zeros[:, 0:1],
                saturate=False,
            )

        def store8(tt):
            nc.sync.dma_start(out=o1[tt:TOK:TT, :], in_=o8[tt][:].bitcast(U8))

        nc.scalar.dma_start(out=twu[:], in_=tw_up.rearrange("b (m t) -> (b m) t", t=TT))
        nc.scalar.dma_start(out=twg[:], in_=tw_gate.rearrange("b (m t) -> (b m) t", t=TT))
        nc.vector.memset(zeros[:], 0.0)
        nc.scalar.activation(out=junk[:], in_=zeros[:], func=ACT.Silu)
        make_identity(nc, ident_f[:])
        make_identity(nc, ident_b[:])

        load_unit(0)
        load_x(0)
        load_unit(1)
        nc.sync.dma_start(
            out=xag[:], in_=xa_gate.flatten_outer_dims().rearrange("(p t) r -> p t r", t=TT)
        )
        nc.sync.dma_start(
            out=xau[:], in_=xa_up.flatten_outer_dims().rearrange("(p t) r -> p t r", t=TT)
        )
        load_unit(2)
        load_b(nc.sync, 0)
        load_unit(3)
        load_x(1)
        load_unit(4)
        load_x(2)
        load_unit(5)
        load_unit(6)
        load_x(3)
        load_b(nc.sync, 1)
        load_unit(7)

        def ok(i):
            return 0 <= i < NTILE

        def last(i):
            return NTILE - TT <= i < NTILE

        def late(i):
            return i + 5 < NUNIT

        def next_load(q):
            nq = q + RAW_BUFS
            if nq < NUNIT:
                load_unit(nq)
                if nq % NU == 0:
                    load_b(nc.sync, nq // NU)

        interleave(0, "V")
        interleave(0, "S")
        next_load(0)
        x_transpose(0)
        x_copy(0)
        quantize(0)
        interleave(1, "V")
        interleave(1, "S")
        next_load(1)
        quant_x(0)
        prep_adapters()
        quantize(1)
        interleave(2, "V")
        interleave(2, "S")
        next_load(2)
        lora_pe(0)
        s12(0)
        quantize(2)
        interleave(3, "V")
        interleave(3, "S")
        next_load(3)
        lora_pe(1)
        s12(1)
        x_transpose(1)
        x_copy(1)
        quantize(3)
        mm(0)
        x_transpose(2)
        lora_pe(2)
        interleave(4, "V")
        interleave(4, "G")
        interleave(4, "S")
        next_load(4)
        quant_x(1)
        x_copy(2)
        v1(0)
        for s in range(0, NTILE + 3):
            qq = s + 4
            qi = s + 5
            if qi < NUNIT and through(qi):
                interleave(qi, "V")
            if s == 1:
                v3(0)
            if qq < NUNIT:
                quantize(qq)
            if s <= 1:
                quant_x(s + 2)
            if qi < NUNIT:
                interleave(qi, "G")
            if ok(s - 1) and late(s - 1) and s != 1:
                v3(s - 1)
            if ok(s + 1):
                mm(s + 1)
            if s == 0:
                x_transpose(3)
            if qi < NUNIT:
                if through(qi):
                    pass_s(qi)
                interleave(qi, "S")
            if through(qi + 1):
                pass_pe(qi + 1)
            if ok(s + 3):
                lora_pe(s + 3)
            if ok(s):
                s3(s)
            if qi < NUNIT and not through(qi):
                interleave(qi, "V")
            if ok(s):
                v2(s)
            if s - 2 == NTILE - 1:
                cast_v(TT - 2, 3 * CAST_PIECE, cast_cols(TT - 2))
                store8(TT - 2)
            if ok(s + 2):
                s12(s + 2)
            if s == 0:
                x_copy(3)
            if ok(s + 1):
                v1(s + 1)
            if ok(s - 1):
                v4(s - 1)
            woven = s - 2 == NTILE - 2
            held = s - 2 == NTILE - TT
            if last(s - 2):
                if not held:
                    cast_v((s - 2) % TT, 0, CAST_PIECE if woven else cast_cols((s - 2) % TT))
                else:
                    o8[0] = o8p.tile([P, HID], FP8, name="o8")
                cast_s((s - 2) % TT)
                if not woven and not held:
                    store8((s - 2) % TT)
            if last(s - 1):
                fin_b((s - 1) % TT)
            if woven:
                cast_v(TT - 2, CAST_PIECE, 2 * CAST_PIECE)
            if qi < NUNIT:
                next_load(qi)
            if ok(s) and not late(s):
                v3(s)
            if last(s - 1):
                fin_c((s - 1) % TT)
            if held:
                cast_v(0, 0, cast_cols(0))
                store8(0)
            if woven:
                cast_v(TT - 2, 2 * CAST_PIECE, 3 * CAST_PIECE)
